import numpy as np
import ml_dtypes


BF16 = ml_dtypes.bfloat16


def bf(x):
    return np.asarray(x, np.float32).astype(BF16)


def f64(x):
    return np.asarray(x).astype(np.float64)


E2M1 = np.array([0.0, 0.5, 1.0, 1.5, 2.0, 3.0, 4.0, 6.0, -0.0, -0.5, -1.0, -1.5, -2.0, -3.0, -4.0, -6.0])


def pack_weight(w, fmt):
    k, n = w.shape
    w = f64(bf(w)).reshape(k // 32, 32, n)
    amax = np.abs(w).max(1)
    if fmt == "e4m3":
        byte = np.frexp(amax)[1] - 1 + 127 - 7
    else:
        mant, ex = np.frexp(amax / 6.0)
        byte = np.where(mant > 0.5, ex, ex - 1) + 127
    byte = np.clip(np.where(amax > 0, byte, 1), 1, 254)
    scaled = (w * np.exp2(127.0 - byte)[:, None, :]).reshape(k, n).astype(np.float32)
    by_word = np.ascontiguousarray(scaled.reshape(k // 512, 128, 4, n).transpose(0, 1, 3, 2))
    if fmt == "e4m3":
        words = by_word.astype(ml_dtypes.float8_e4m3fn).view(np.uint8)
    else:
        c = by_word.astype(ml_dtypes.float4_e2m1fn).view(np.uint8) & 0xF
        words = c[..., 0::2] | (c[..., 1::2] << 4)
    return np.ascontiguousarray(words), np.ascontiguousarray(byte.astype(np.uint8).reshape(k // 512, 16, n))


def unpack_weight(words, scales, fmt):
    g, p, n, _ = words.shape
    if fmt == "e4m3":
        vals = np.ascontiguousarray(words).view(ml_dtypes.float8_e4m3fn).astype(np.float64)
    else:
        nib = np.empty((g, p, n, 4), np.uint8)
        nib[..., 0::2] = words & 0xF
        nib[..., 1::2] = words >> 4
        vals = E2M1[nib]
    vals = vals * np.repeat(np.exp2(scales.astype(np.float64) - 127.0), 8, axis=1)[..., None]
    return vals.transpose(0, 1, 3, 2).reshape(g * 512, n)

def pack4(w):
    words, scales = pack_weight(w, "e2m1")
    return words.reshape(words.shape[0], 128, -1), scales


def unpack4(words, scales):
    return unpack_weight(words.reshape(words.shape[0], 128, -1, 2), scales, "e2m1")


def kspread(k):
    return np.exp2(np.repeat(np.random.randint(-6, 7, k // 32), 32).astype(np.float64))


B, T, C, H, NOPE, ROPE, VD, LORA = 1, 2048, 2048, 16, 128, 128, 128, 512
QK = NOPE + ROPE
HALF = ROPE // 2


def make_freq_cis():
    inv = 1.0 / (10000.0 ** (np.arange(0, ROPE, 2) / ROPE))
    ang = np.outer(np.arange(T), inv)
    return np.stack([np.cos(ang), np.sin(ang)], -1)


def apply_rope(v, fc):
    vr = v.reshape(B, T, H, HALF, 2)
    f = fc.reshape(1, T, 1, HALF, 2)
    real = vr[..., 0] * f[..., 0] - vr[..., 1] * f[..., 1]
    imag = vr[..., 1] * f[..., 0] + vr[..., 0] * f[..., 1]
    return np.stack([real, imag], -1).reshape(B, T, H, ROPE)


def setup_inputs():
    s = kspread(C)
    x = np.random.standard_normal((B, T, C)) * s
    x_words, x_scales = pack4(np.ascontiguousarray(x.reshape(B * T, C).T))
    freq_cis = bf(make_freq_cis())
    words, scales = pack4(np.random.standard_normal((C, H * QK)) * 2.0 / np.sqrt(C) / s[:, None])
    return {"x_words": x_words,
            "x_scales": x_scales,
            "freq_cis": freq_cis,
            "Wq_words": words,
            "Wq_scales": scales}


def reference(x_words, x_scales, freq_cis, Wq_words, Wq_scales):
    q = (unpack4(x_words, x_scales).T.reshape(B, T, C) @ unpack4(Wq_words, Wq_scales)).reshape(B, T, H, QK)
    q_nope, q_rope = q[..., :NOPE], q[..., NOPE:]
    q_rope = apply_rope(q_rope, f64(freq_cis))
    return np.concatenate([q_nope, q_rope], -1)

@@ -1,0 +1,276 @@
+from contextlib import ExitStack
+
+import concourse.mybir as mybir
+
+F32 = mybir.dt.float32
+BF16 = mybir.dt.bfloat16
+U8 = mybir.dt.uint8
+I32 = mybir.dt.int32
+FP4X4 = mybir.dt.float4_e2m1fn_x4
+MULT = mybir.AluOpType.mult
+ADD = mybir.AluOpType.add
+
+P = 128
+TOKENS = 2048
+K = 2048
+FEATURES = 4096
+PASSES = K // 512
+M_TILES = TOKENS // P
+N_TILE = 512
+N_BLOCKS = FEATURES // N_TILE
+HEADS = 2
+PAIR = 2
+TAIL = 4
+WARM_FREE = 4
+WARM_TIED = 5
+WARM_LAST = 2
+
+FLOPS = 2 * TOKENS * K * FEATURES
+
+X_SCALE_CHUNKS = [(0, 4), (4, 4), (8, 8)]
+X_CODE_CHUNKS = [(0, 2), (2, 2), (4, 4), (8, 4), (12, 4)]
+W_SCALE_CHUNKS = [(0, 1), (1, 1), (2, 2), (4, 2), (6, 2)]
+W_CODE_CHUNKS = [(0, 1), (1, 1), (2, 2), (4, 2), (6, 2)]
+ROWS = (0, 1, 2, 3)
+LATER_W = {8: 2, 24: 3, 40: 4}
+REGROUP_AT = 64
+
+
+def find_chunk(chunks, index):
+    for c, (first, count) in enumerate(chunks):
+        if first <= index < first + count:
+            return c, index - first
+    raise ValueError("index outside the chunks")
+
+
+def tile_multiheadlatentattention_pb_kernel(tc, x_words, x_scales, freq_cis, Wq_words, Wq_scales, out):
+    nc = tc.nc
+    out_v = out.rearrange("b (m p) h d -> p (b m) (h d)", p=P)
+    last_n = N_BLOCKS - 1
+
+    with ExitStack() as ctx:
+        keep = ctx.enter_context(tc.tile_pool(name="keep", bufs=1))
+        prod = ctx.enter_context(tc.tile_pool(name="prod", bufs=4))
+        res = ctx.enter_context(tc.tile_pool(name="res", bufs=20))
+        psum = ctx.enter_context(tc.psum_pool(name="psum", bufs=8))
+        ctx.enter_context(tc.manual_schedule())
+
+        xs = [keep.tile([P, PASSES, P * n], U8, name="xs%d" % i, align_bytes=64) for i, (f, n) in enumerate(X_SCALE_CHUNKS)]
+        xc = [keep.tile([P, PASSES, 2 * P * n], U8, name="xc%d" % i, align_bytes=64) for i, (f, n) in enumerate(X_CODE_CHUNKS)]
+        ws = [keep.tile([P, PASSES, N_TILE * n], U8, name="ws%d" % i, align_bytes=64) for i, (f, n) in enumerate(W_SCALE_CHUNKS)]
+        wc = [keep.tile([P, PASSES, 2 * N_TILE * n], U8, name="wc%d" % i, align_bytes=64) for i, (f, n) in enumerate(W_CODE_CHUNKS)]
+        ws_last = keep.tile([P, PASSES, N_TILE], U8, name="ws_last", align_bytes=64)
+        wc_last = keep.tile([P, PASSES, 2 * N_TILE], U8, name="wc_last", align_bytes=64)
+        fc = keep.tile([P, M_TILES, P], BF16, name="fc")
+        table = keep.tile([P, M_TILES, 2 * P], BF16, name="table")
+        zeros = keep.tile([P, N_TILE], BF16, name="zeros")
+        tied = keep.tile([P, P], BF16, name="tied")
+        tied_last = keep.tile([P, P], BF16, name="tied_last")
+        act_in = keep.tile([P, 8], F32, name="act_in")
+        act_out = keep.tile([P, 8], F32, name="act_out")
+
+        def load_codes(tile, words, chunk, unit):
+            first, count = chunk
+            nc.sync.dma_start(
+                out=tile[:].bitcast(I32),
+                in_=words[:, :, unit * first : unit * (first + count)].rearrange("g p b -> p g b").bitcast(I32),
+            )
+
+        def load_scales(tile, scales, chunk, unit, rows):
+            first, count = chunk
+            for r in rows:
+                nc.sync.dma_start(
+                    out=tile[r:P:32, :, :].bitcast(I32),
+                    in_=scales[:, r:16:4, unit * first : unit * (first + count)].rearrange("g q n -> q g n").bitcast(I32),
+                )
+
+        def load_x_scales(i, rows=ROWS):
+            load_scales(xs[i], x_scales, X_SCALE_CHUNKS[i], P, rows)
+
+        def load_x_codes(i):
+            load_codes(xc[i], x_words, X_CODE_CHUNKS[i], 2 * P)
+
+        def load_w_scales(i):
+            load_scales(ws[i], Wq_scales, W_SCALE_CHUNKS[i], N_TILE, ROWS)
+
+        def load_w_codes(i):
+            load_codes(wc[i], Wq_words, W_CODE_CHUNKS[i], 2 * N_TILE)
+
+        fc_src = freq_cis.rearrange("(m p) i e -> p m (i e)", p=P)
+
+        def load_fc(i):
+            nc.sync.dma_start(out=fc[:, 4 * i : 4 * i + 4, :], in_=fc_src[:, 4 * i : 4 * i + 4, :])
+
+        nc.gpsimd.memset(zeros[:], 0.0)
+        nc.gpsimd.memset(act_in[:], 0.0)
+        nc.scalar.copy(out=act_out[:], in_=act_in[:])
+
+        for t in (ws[0], xs[0], xs[1], xs[2]):
+            nc.vector.memset(t[:].bitcast(I32), 0)
+
+        load_w_scales(0)
+        load_x_scales(0, (0, 1))
+        load_w_codes(0)
+        load_x_codes(0)
+        load_x_scales(0, (2, 3))
+        load_x_codes(1)
+        load_x_codes(2)
+        load_x_scales(1)
+        load_fc(0)
+        load_fc(1)
+        load_x_scales(2)
+        load_x_codes(3)
+        load_fc(2)
+        load_x_codes(4)
+        load_fc(3)
+
+        warm = psum.tile([P, N_TILE], F32, name="acc")
+        for i in range(WARM_FREE):
+            nc.tensor.matmul(out=warm[:], lhsT=zeros[:, 0:P], rhs=zeros[:], start=True, stop=True)
+        nc.vector.tensor_scalar(out=tied[:], in0=ws[0][:, 0, :].bitcast(I32), scalar1=0.0, scalar2=None, op0=MULT)
+        for i in range(WARM_TIED):
+            nc.tensor.matmul(out=warm[:], lhsT=tied[:], rhs=zeros[:], start=True, stop=True)
+        nc.vector.memset(ws[1][:].bitcast(I32), 0)
+        nc.vector.tensor_scalar(
+            out=tied_last[:], in0=wc[0][:, PASSES - 1, 0 : 4 * P].bitcast(I32), scalar1=0.0, scalar2=None, op0=MULT
+        )
+        for i in range(WARM_LAST):
+            nc.tensor.matmul(out=warm[:], lhsT=tied_last[:], rhs=zeros[:], start=True, stop=True)
+        load_w_scales(1)
+        load_w_codes(1)
+
+        fc_v = fc[:].rearrange("p m (i e) -> p m i e", e=2)
+        table_v = table[:].rearrange("p m (i q e) -> p m i q e", q=2, e=2)
+
+        def build_table(i):
+            m0, m1 = 4 * i, 4 * i + 4
+            nc.vector.tensor_copy(out=table_v[:, m0:m1, :, 0, :], in_=fc_v[:, m0:m1, :, :])
+            nc.vector.tensor_scalar(
+                out=table_v[:, m0:m1, :, 1, 0], in0=fc_v[:, m0:m1, :, 1], scalar1=-1.0, scalar2=None, op0=MULT
+            )
+            nc.vector.tensor_copy(out=table_v[:, m0:m1, :, 1, 1], in_=fc_v[:, m0:m1, :, 0])
+
+        def regroup_last_block():
+            wci, wcn = find_chunk(W_CODE_CHUNKS, last_n)
+            wsi, wsn = find_chunk(W_SCALE_CHUNKS, last_n)
+            moves = (
+                (wc_last, wc[wci][:, :, 2 * N_TILE * wcn : 2 * N_TILE * (wcn + 1)]),
+                (ws_last, ws[wsi][:, :, N_TILE * wsn : N_TILE * (wsn + 1)]),
+            )
+            for dst, src in moves:
+                src_v = src.bitcast(I32).rearrange("p g (h k w) -> p g h k w", h=HEADS, k=2)
+                dst_v = dst[:].bitcast(I32).rearrange("p g (k h w) -> p g k h w", k=2, h=HEADS)
+                nc.vector.tensor_copy(out=dst_v[:, :, 0, :, :], in_=src_v[:, :, :, 1, :])
+                nc.vector.tensor_copy(out=dst_v[:, :, 1, :, :], in_=src_v[:, :, :, 0, :])
+
+        def mx_group(acc, m, n, col0, width):
+            xci, xcm = find_chunk(X_CODE_CHUNKS, m)
+            xsi, xsm = find_chunk(X_SCALE_CHUNKS, m)
+            if n == last_n:
+                w_codes, w_scales, code_col, scale_col = wc_last, ws_last, col0, col0
+            else:
+                wci, wcn = find_chunk(W_CODE_CHUNKS, n)
+                wsi, wsn = find_chunk(W_SCALE_CHUNKS, n)
+                w_codes, w_scales = wc[wci], ws[wsi]
+                code_col, scale_col = N_TILE * wcn + col0, N_TILE * wsn + col0
+            for g in range(PASSES):
+                nc.tensor.matmul_mx(
+                    out=acc,
+                    lhsT=xc[xci][:, g, 2 * P * xcm : 2 * P * (xcm + 1)].bitcast(FP4X4),
+                    lhsT_scale=xs[xsi][:, g, P * xsm : P * (xsm + 1)],
+                    rhs=w_codes[:, g, 2 * code_col : 2 * (code_col + width)].bitcast(FP4X4),
+                    rhs_scale=w_scales[:, g, scale_col : scale_col + width],
+                    start=(g == 0),
+                    stop=(g == PASSES - 1),
+                )
+
+        def by_head(ap):
+            return ap.rearrange("p (h d) -> p h d", h=HEADS)
+
+        def rope_products(ab_bank, rope, m):
+            nc.vector.tensor_tensor(
+                out=ab_bank.rearrange("p (h k e) -> p h k e", h=HEADS, e=2),
+                in0=rope.unsqueeze(3).to_broadcast([P, HEADS, P, 2]),
+                in1=table[:, m, :].rearrange("p (k e) -> p k e", e=2).unsqueeze(1).to_broadcast([P, HEADS, P, 2]),
+                op=MULT,
+            )
+
+        def rope_sums(engine, ab, o, first, count):
+            ab_v = ab[:, first : first + count, :].rearrange("p j (h i q e) -> p (j h) i q e", h=HEADS, q=2, e=2)
+            o_v = (
+                o[:, first : first + count, :]
+                .rearrange("p j (h d) -> p (j h) d", h=HEADS)[:, :, P : 2 * P]
+                .rearrange("p a (i e) -> p a i e", e=2)
+            )
+            engine.tensor_tensor(out=o_v, in0=ab_v[:, :, :, 0, :], in1=ab_v[:, :, :, 1, :], op=ADD)
+
+        def finish_pair(ab, o, m, n):
+            rope_sums(nc.gpsimd, ab, o, 0, PAIR)
+            nc.sync.dma_start(out=out_v[:, m : m + PAIR, N_TILE * n : N_TILE * (n + 1)], in_=o[:])
+
+        def finish_rope(ab, o, half, m):
+            rope_sums(nc.vector, ab, o, half, 1)
+            nc.sync.dma_start(
+                out=by_head(out_v[:, m, N_TILE * last_n : N_TILE * (last_n + 1)])[:, :, P : 2 * P],
+                in_=by_head(o[:, half, :])[:, :, P : 2 * P],
+            )
+
+        build_table(0)
+        pending = None
+        ab = None
+        o = None
+        for j in range(N_BLOCKS * M_TILES - TAIL):
+            n, m = divmod(j, M_TILES)
+            half = j % PAIR
+            acc = psum.tile([P, N_TILE], F32, name="acc")
+            mx_group(acc[:], m, n, 0, N_TILE)
+            if half == 0:
+                ab = prod.tile([P, PAIR, N_TILE], F32, name="ab")
+                o = res.tile([P, PAIR, N_TILE], F32, name="o")
+            if n == last_n:
+                rope, nope = by_head(acc[:, 0 : N_TILE // 2]), by_head(acc[:, N_TILE // 2 : N_TILE])
+            else:
+                rope, nope = by_head(acc[:])[:, :, P : 2 * P], by_head(acc[:])[:, :, 0:P]
+            rope_products(ab[:, half, :], rope, m)
+            nc.scalar.copy(out=by_head(o[:, half, :])[:, :, 0:P], in_=nope)
+            if pending is not None:
+                finish_pair(*pending)
+                pending = None
+            if half == PAIR - 1:
+                pending = (ab, o, m - (PAIR - 1), n)
+            if n == 0 and m in (1, 5, 9):
+                build_table((m + 3) // 4)
+            if j in LATER_W:
+                nc.vector.memset(ws[LATER_W[j]][:].bitcast(I32), 0)
+                load_w_scales(LATER_W[j])
+                load_w_codes(LATER_W[j])
+            if j == REGROUP_AT:
+                regroup_last_block()
+
+        tail = []
+        for t in range(TAIL):
+            m = M_TILES - TAIL + t
+            half = t % PAIR
+            acc = psum.tile([P, N_TILE], F32, name="acc")
+            mx_group(acc[:, 0 : N_TILE // 2], m, last_n, 0, N_TILE // 2)
+            if half == 0:
+                ab = prod.tile([P, PAIR, N_TILE], F32, name="ab")
+                o = res.tile([P, PAIR, N_TILE], F32, name="o")
+            rope_products(ab[:, half, :], by_head(acc[:, 0 : N_TILE // 2]), m)
+            if t == 0:
+                finish_pair(*pending)
+            else:
+                finish_rope(*tail[t - 1])
+            tail.append((ab, o, half, m))
+        finish_rope(*tail[TAIL - 1])
+        for ab, o, half, m in tail:
+            acc = psum.tile([P, N_TILE], F32, name="acc")
+            mx_group(acc[:, 0 : N_TILE // 2], m, last_n, N_TILE // 2, N_TILE // 2)
+            kept = by_head(o[:, half, :])[:, :, 0:P]
+            kept_out = by_head(out_v[:, m, N_TILE * last_n : N_TILE * (last_n + 1)])[:, :, 0:P]
+            if m < M_TILES - 1:
+                nc.scalar.copy(out=kept, in_=by_head(acc[:, 0 : N_TILE // 2]))
+                nc.scalar.dma_start(out=kept_out, in_=kept)
+            else:
+                nc.vector.tensor_copy(out=kept, in_=by_head(acc[:, 0 : N_TILE // 2]))
+                nc.sync.dma_start(out=kept_out, in_=kept)

@@ -23,11 +23,10 @@ PAIR = 2
 TAIL = 4
 WARM_FREE = 4
 WARM_TIED = 5
-WARM_LAST = 2
 
 FLOPS = 2 * TOKENS * K * FEATURES
 
-X_SCALE_CHUNKS = [(0, 4), (4, 4), (8, 8)]
+X_SCALE_CHUNKS = [(0, 2), (2, 6), (8, 8)]
 X_CODE_CHUNKS = [(0, 2), (2, 2), (4, 4), (8, 4), (12, 4)]
 W_SCALE_CHUNKS = [(0, 1), (1, 1), (2, 2), (4, 2), (6, 2)]
 W_CODE_CHUNKS = [(0, 1), (1, 1), (2, 2), (4, 2), (6, 2)]
@@ -65,7 +64,6 @@ def tile_multiheadlatentattention_pb_kernel(tc, x_words, x_scales, freq_cis, Wq_
         table = keep.tile([P, M_TILES, 2 * P], BF16, name="table")
         zeros = keep.tile([P, N_TILE], BF16, name="zeros")
         tied = keep.tile([P, P], BF16, name="tied")
-        tied_last = keep.tile([P, P], BF16, name="tied_last")
         act_in = keep.tile([P, 8], F32, name="act_in")
         act_out = keep.tile([P, 8], F32, name="act_out")
 
@@ -101,21 +99,23 @@ def tile_multiheadlatentattention_pb_kernel(tc, x_words, x_scales, freq_cis, Wq_
         def load_fc(i):
             nc.sync.dma_start(out=fc[:, 4 * i : 4 * i + 4, :], in_=fc_src[:, 4 * i : 4 * i + 4, :])
 
-        nc.gpsimd.memset(zeros[:], 0.0)
+        nc.gpsimd.memset(xs[0][:].bitcast(F32), 0.0)
         nc.gpsimd.memset(act_in[:], 0.0)
         nc.scalar.copy(out=act_out[:], in_=act_in[:])
 
-        for t in (ws[0], xs[0], xs[1], xs[2]):
+        nc.vector.memset(zeros[:], 0.0)
+        for t in (ws[0], xs[1], xs[2]):
             nc.vector.memset(t[:].bitcast(I32), 0)
+        nc.vector.memset(tied[:], 0.0)
 
-        load_w_scales(0)
         load_x_scales(0, (0, 1))
         load_w_codes(0)
         load_x_codes(0)
+        load_w_scales(0)
         load_x_scales(0, (2, 3))
         load_x_codes(1)
-        load_x_codes(2)
         load_x_scales(1)
+        load_x_codes(2)
         load_fc(0)
         load_fc(1)
         load_x_scales(2)
@@ -127,15 +127,16 @@ def tile_multiheadlatentattention_pb_kernel(tc, x_words, x_scales, freq_cis, Wq_
         warm = psum.tile([P, N_TILE], F32, name="acc")
         for i in range(WARM_FREE):
             nc.tensor.matmul(out=warm[:], lhsT=zeros[:, 0:P], rhs=zeros[:], start=True, stop=True)
-        nc.vector.tensor_scalar(out=tied[:], in0=ws[0][:, 0, :].bitcast(I32), scalar1=0.0, scalar2=None, op0=MULT)
+        nc.vector.tensor_scalar(
+            out=tied[0:1, :],
+            in0=xs[0][0:1, 0:2, :].rearrange("p g n -> p (g n)").bitcast(I32),
+            scalar1=0.0,
+            scalar2=None,
+            op0=MULT,
+        )
         for i in range(WARM_TIED):
             nc.tensor.matmul(out=warm[:], lhsT=tied[:], rhs=zeros[:], start=True, stop=True)
         nc.vector.memset(ws[1][:].bitcast(I32), 0)
-        nc.vector.tensor_scalar(
-            out=tied_last[:], in0=wc[0][:, PASSES - 1, 0 : 4 * P].bitcast(I32), scalar1=0.0, scalar2=None, op0=MULT
-        )
-        for i in range(WARM_LAST):
-            nc.tensor.matmul(out=warm[:], lhsT=tied_last[:], rhs=zeros[:], start=True, stop=True)
         load_w_scales(1)
         load_w_codes(1)
 

@@ -22,7 +22,7 @@ HEADS = 2
 PAIR = 2
 TAIL = 4
 WARM_FREE = 4
-WARM_TIED = 5
+WARM_TIED = 9
 
 FLOPS = 2 * TOKENS * K * FEATURES
 

@@ -48,18 +48,20 @@ def tile_multiheadlatentattention_pb_kernel(tc, x_words, x_scales, freq_cis, Wq_
     last_n = N_BLOCKS - 1
 
     with ExitStack() as ctx:
+        x_ops = ctx.enter_context(tc.tile_pool(name="x_ops", bufs=1))
         keep = ctx.enter_context(tc.tile_pool(name="keep", bufs=1))
         prod = ctx.enter_context(tc.tile_pool(name="prod", bufs=4))
         res = ctx.enter_context(tc.tile_pool(name="res", bufs=20))
+        w_ops = ctx.enter_context(tc.tile_pool(name="w_ops", bufs=1))
         psum = ctx.enter_context(tc.psum_pool(name="psum", bufs=8))
         ctx.enter_context(tc.manual_schedule())
 
-        xs = [keep.tile([P, PASSES, P * n], U8, name="xs%d" % i, align_bytes=64) for i, (f, n) in enumerate(X_SCALE_CHUNKS)]
-        xc = [keep.tile([P, PASSES, 2 * P * n], U8, name="xc%d" % i, align_bytes=64) for i, (f, n) in enumerate(X_CODE_CHUNKS)]
-        ws = [keep.tile([P, PASSES, N_TILE * n], U8, name="ws%d" % i, align_bytes=64) for i, (f, n) in enumerate(W_SCALE_CHUNKS)]
-        wc = [keep.tile([P, PASSES, 2 * N_TILE * n], U8, name="wc%d" % i, align_bytes=64) for i, (f, n) in enumerate(W_CODE_CHUNKS)]
-        ws_last = keep.tile([P, PASSES, N_TILE], U8, name="ws_last", align_bytes=64)
-        wc_last = keep.tile([P, PASSES, 2 * N_TILE], U8, name="wc_last", align_bytes=64)
+        xs = [x_ops.tile([P, PASSES, P * n], U8, name="xs%d" % i, align_bytes=64) for i, (f, n) in enumerate(X_SCALE_CHUNKS)]
+        xc = [x_ops.tile([P, PASSES, 2 * P * n], U8, name="xc%d" % i, align_bytes=64) for i, (f, n) in enumerate(X_CODE_CHUNKS)]
+        ws = [w_ops.tile([P, PASSES, N_TILE * n], U8, name="ws%d" % i, align_bytes=64) for i, (f, n) in enumerate(W_SCALE_CHUNKS)]
+        wc = [w_ops.tile([P, PASSES, 2 * N_TILE * n], U8, name="wc%d" % i, align_bytes=64) for i, (f, n) in enumerate(W_CODE_CHUNKS)]
+        ws_last = w_ops.tile([P, PASSES, N_TILE], U8, name="ws_last", align_bytes=64)
+        wc_last = w_ops.tile([P, PASSES, 2 * N_TILE], U8, name="wc_last", align_bytes=64)
         fc = keep.tile([P, M_TILES, P], BF16, name="fc")
         table = keep.tile([P, M_TILES, 2 * P], BF16, name="table")
         zeros = keep.tile([P, N_TILE], BF16, name="zeros")

@@ -241,6 +241,8 @@ def tile_multiheadlatentattention_pb_kernel(tc, x_words, x_scales, freq_cis, Wq_
                 pending = None
             if half == PAIR - 1:
                 pending = (ab, o, m - (PAIR - 1), n)
+            if j == N_BLOCKS * M_TILES - TAIL - 1:
+                rope_sums(nc.gpsimd, ab, o, 0, 1)
             if n == 0 and m in (1, 5, 9):
                 build_table((m + 3) // 4)
             if j in LATER_W:
@@ -261,7 +263,10 @@ def tile_multiheadlatentattention_pb_kernel(tc, x_words, x_scales, freq_cis, Wq_
                 o = res.tile([P, PAIR, N_TILE], F32, name="o")
             rope_products(ab[:, half, :], by_head(acc[:, 0 : N_TILE // 2]), m)
             if t == 0:
-                finish_pair(*pending)
+                rope_sums(nc.gpsimd, pending[0], pending[1], 1, 1)
+                nc.sync.dma_start(
+                    out=out_v[:, pending[2] : pending[2] + PAIR, N_TILE * last_n : N_TILE * (last_n + 1)], in_=pending[1][:]
+                )
             else:
                 finish_rope(*tail[t - 1])
             tail.append((ab, o, half, m))

@@ -22,7 +22,7 @@ HEADS = 2
 PAIR = 2
 TAIL = 4
 WARM_FREE = 4
-WARM_TIED = 9
+WARM_TIED = 7
 
 FLOPS = 2 * TOKENS * K * FEATURES
 
@@ -110,9 +110,9 @@ def tile_multiheadlatentattention_pb_kernel(tc, x_words, x_scales, freq_cis, Wq_
             nc.vector.memset(t[:].bitcast(I32), 0)
         nc.vector.memset(tied[:], 0.0)
 
+        load_x_codes(0)
         load_x_scales(0, (0, 1))
         load_w_codes(0)
-        load_x_codes(0)
         load_w_scales(0)
         load_x_scales(0, (2, 3))
         load_x_codes(1)

@@ -268,17 +268,19 @@ def tile_multiheadlatentattention_pb_kernel(tc, x_words, x_scales, freq_cis, Wq_
                     out=out_v[:, pending[2] : pending[2] + PAIR, N_TILE * last_n : N_TILE * (last_n + 1)], in_=pending[1][:]
                 )
             else:
-                finish_rope(*tail[t - 1])
+                rope_sums(nc.vector, tail[t - 1][0], tail[t - 1][1], tail[t - 1][2], 1)
             tail.append((ab, o, half, m))
-        finish_rope(*tail[TAIL - 1])
         for ab, o, half, m in tail:
+            if m == M_TILES - 2:
+                finish_rope(*tail[TAIL - 1])
             acc = psum.tile([P, N_TILE], F32, name="acc")
             mx_group(acc[:, 0 : N_TILE // 2], m, last_n, N_TILE // 2, N_TILE // 2)
             kept = by_head(o[:, half, :])[:, :, 0:P]
-            kept_out = by_head(out_v[:, m, N_TILE * last_n : N_TILE * (last_n + 1)])[:, :, 0:P]
             if m < M_TILES - 1:
                 nc.scalar.copy(out=kept, in_=by_head(acc[:, 0 : N_TILE // 2]))
-                nc.scalar.dma_start(out=kept_out, in_=kept)
+                nc.sync.dma_start(out=out_v[:, m, N_TILE * last_n : N_TILE * (last_n + 1)], in_=o[:, half, :])
             else:
                 nc.vector.tensor_copy(out=kept, in_=by_head(acc[:, 0 : N_TILE // 2]))
-                nc.sync.dma_start(out=kept_out, in_=kept)
+                nc.sync.dma_start(
+                    out=by_head(out_v[:, m, N_TILE * last_n : N_TILE * (last_n + 1)])[:, :, 0:P], in_=kept
+                )

@@ -211,13 +211,6 @@ def tile_multiheadlatentattention_pb_kernel(tc, x_words, x_scales, freq_cis, Wq_
             rope_sums(nc.gpsimd, ab, o, 0, PAIR)
             nc.sync.dma_start(out=out_v[:, m : m + PAIR, N_TILE * n : N_TILE * (n + 1)], in_=o[:])
 
-        def finish_rope(ab, o, half, m):
-            rope_sums(nc.vector, ab, o, half, 1)
-            nc.sync.dma_start(
-                out=by_head(out_v[:, m, N_TILE * last_n : N_TILE * (last_n + 1)])[:, :, P : 2 * P],
-                in_=by_head(o[:, half, :])[:, :, P : 2 * P],
-            )
-
         build_table(0)
         pending = None
         ab = None
@@ -270,17 +263,9 @@ def tile_multiheadlatentattention_pb_kernel(tc, x_words, x_scales, freq_cis, Wq_
             else:
                 rope_sums(nc.vector, tail[t - 1][0], tail[t - 1][1], tail[t - 1][2], 1)
             tail.append((ab, o, half, m))
+        rope_sums(nc.vector, tail[TAIL - 1][0], tail[TAIL - 1][1], tail[TAIL - 1][2], 1)
         for ab, o, half, m in tail:
-            if m == M_TILES - 2:
-                finish_rope(*tail[TAIL - 1])
             acc = psum.tile([P, N_TILE], F32, name="acc")
             mx_group(acc[:, 0 : N_TILE // 2], m, last_n, N_TILE // 2, N_TILE // 2)
-            kept = by_head(o[:, half, :])[:, :, 0:P]
-            if m < M_TILES - 1:
-                nc.scalar.copy(out=kept, in_=by_head(acc[:, 0 : N_TILE // 2]))
-                nc.sync.dma_start(out=out_v[:, m, N_TILE * last_n : N_TILE * (last_n + 1)], in_=o[:, half, :])
-            else:
-                nc.vector.tensor_copy(out=kept, in_=by_head(acc[:, 0 : N_TILE // 2]))
-                nc.sync.dma_start(
-                    out=by_head(out_v[:, m, N_TILE * last_n : N_TILE * (last_n + 1)])[:, :, 0:P], in_=kept
-                )
+            nc.scalar.copy(out=by_head(o[:, half, :])[:, :, 0:P], in_=by_head(acc[:, 0 : N_TILE // 2]))
+            nc.sync.dma_start(out=out_v[:, m, N_TILE * last_n : N_TILE * (last_n + 1)], in_=o[:, half, :])

from contextlib import ExitStack

import concourse.mybir as mybir

F32 = mybir.dt.float32
BF16 = mybir.dt.bfloat16
U8 = mybir.dt.uint8
I32 = mybir.dt.int32
FP4X4 = mybir.dt.float4_e2m1fn_x4
MULT = mybir.AluOpType.mult
ADD = mybir.AluOpType.add

P = 128
TOKENS = 2048
K = 2048
FEATURES = 4096
PASSES = K // 512
M_TILES = TOKENS // P
N_TILE = 512
N_BLOCKS = FEATURES // N_TILE
HEADS = 2
PAIR = 2
TAIL = 4
WARM_FREE = 4
WARM_TIED = 7

FLOPS = 2 * TOKENS * K * FEATURES

X_SCALE_CHUNKS = [(0, 2), (2, 6), (8, 8)]
X_CODE_CHUNKS = [(0, 2), (2, 2), (4, 4), (8, 4), (12, 4)]
W_SCALE_CHUNKS = [(0, 1), (1, 1), (2, 2), (4, 2), (6, 2)]
W_CODE_CHUNKS = [(0, 1), (1, 1), (2, 2), (4, 2), (6, 2)]
ROWS = (0, 1, 2, 3)
LATER_W = {8: 2, 24: 3, 40: 4}
REGROUP_AT = 64


def find_chunk(chunks, index):
    for c, (first, count) in enumerate(chunks):
        if first <= index < first + count:
            return c, index - first
    raise ValueError("index outside the chunks")


def tile_multiheadlatentattention_pb_kernel(tc, x_words, x_scales, freq_cis, Wq_words, Wq_scales, out):
    nc = tc.nc
    out_v = out.rearrange("b (m p) h d -> p (b m) (h d)", p=P)
    last_n = N_BLOCKS - 1

    with ExitStack() as ctx:
        x_ops = ctx.enter_context(tc.tile_pool(name="x_ops", bufs=1))
        keep = ctx.enter_context(tc.tile_pool(name="keep", bufs=1))
        prod = ctx.enter_context(tc.tile_pool(name="prod", bufs=4))
        res = ctx.enter_context(tc.tile_pool(name="res", bufs=20))
        w_ops = ctx.enter_context(tc.tile_pool(name="w_ops", bufs=1))
        psum = ctx.enter_context(tc.psum_pool(name="psum", bufs=8))
        ctx.enter_context(tc.manual_schedule())

        xs = [x_ops.tile([P, PASSES, P * n], U8, name="xs%d" % i, align_bytes=64) for i, (f, n) in enumerate(X_SCALE_CHUNKS)]
        xc = [x_ops.tile([P, PASSES, 2 * P * n], U8, name="xc%d" % i, align_bytes=64) for i, (f, n) in enumerate(X_CODE_CHUNKS)]
        ws = [w_ops.tile([P, PASSES, N_TILE * n], U8, name="ws%d" % i, align_bytes=64) for i, (f, n) in enumerate(W_SCALE_CHUNKS)]
        wc = [w_ops.tile([P, PASSES, 2 * N_TILE * n], U8, name="wc%d" % i, align_bytes=64) for i, (f, n) in enumerate(W_CODE_CHUNKS)]
        ws_last = w_ops.tile([P, PASSES, N_TILE], U8, name="ws_last", align_bytes=64)
        wc_last = w_ops.tile([P, PASSES, 2 * N_TILE], U8, name="wc_last", align_bytes=64)
        fc = keep.tile([P, M_TILES, P], BF16, name="fc")
        table = keep.tile([P, M_TILES, 2 * P], BF16, name="table")
        zeros = keep.tile([P, N_TILE], BF16, name="zeros")
        tied = keep.tile([P, P], BF16, name="tied")
        act_in = keep.tile([P, 8], F32, name="act_in")
        act_out = keep.tile([P, 8], F32, name="act_out")

        def load_codes(tile, words, chunk, unit):
            first, count = chunk
            nc.sync.dma_start(
                out=tile[:].bitcast(I32),
                in_=words[:, :, unit * first : unit * (first + count)].rearrange("g p b -> p g b").bitcast(I32),
            )

        def load_scales(tile, scales, chunk, unit, rows):
            first, count = chunk
            for r in rows:
                nc.sync.dma_start(
                    out=tile[r:P:32, :, :].bitcast(I32),
                    in_=scales[:, r:16:4, unit * first : unit * (first + count)].rearrange("g q n -> q g n").bitcast(I32),
                )

        def load_x_scales(i, rows=ROWS):
            load_scales(xs[i], x_scales, X_SCALE_CHUNKS[i], P, rows)

        def load_x_codes(i):
            load_codes(xc[i], x_words, X_CODE_CHUNKS[i], 2 * P)

        def load_w_scales(i):
            load_scales(ws[i], Wq_scales, W_SCALE_CHUNKS[i], N_TILE, ROWS)

        def load_w_codes(i):
            load_codes(wc[i], Wq_words, W_CODE_CHUNKS[i], 2 * N_TILE)

        fc_src = freq_cis.rearrange("(m p) i e -> p m (i e)", p=P)

        def load_fc(i):
            nc.sync.dma_start(out=fc[:, 4 * i : 4 * i + 4, :], in_=fc_src[:, 4 * i : 4 * i + 4, :])

        nc.gpsimd.memset(xs[0][:].bitcast(F32), 0.0)
        nc.gpsimd.memset(act_in[:], 0.0)
        nc.scalar.copy(out=act_out[:], in_=act_in[:])

        nc.vector.memset(zeros[:], 0.0)
        for t in (ws[0], xs[1], xs[2]):
            nc.vector.memset(t[:].bitcast(I32), 0)
        nc.vector.memset(tied[:], 0.0)

        load_x_codes(0)
        load_x_scales(0, (0, 1))
        load_w_codes(0)
        load_w_scales(0)
        load_x_scales(0, (2, 3))
        load_x_codes(1)
        load_x_scales(1)
        load_x_codes(2)
        load_fc(0)
        load_fc(1)
        load_x_scales(2)
        load_x_codes(3)
        load_fc(2)
        load_x_codes(4)
        load_fc(3)

        warm = psum.tile([P, N_TILE], F32, name="acc")
        for i in range(WARM_FREE):
            nc.tensor.matmul(out=warm[:], lhsT=zeros[:, 0:P], rhs=zeros[:], start=True, stop=True)
        nc.vector.tensor_scalar(
            out=tied[0:1, :],
            in0=xs[0][0:1, 0:2, :].rearrange("p g n -> p (g n)").bitcast(I32),
            scalar1=0.0,
            scalar2=None,
            op0=MULT,
        )
        for i in range(WARM_TIED):
            nc.tensor.matmul(out=warm[:], lhsT=tied[:], rhs=zeros[:], start=True, stop=True)
        nc.vector.memset(ws[1][:].bitcast(I32), 0)
        load_w_scales(1)
        load_w_codes(1)

        fc_v = fc[:].rearrange("p m (i e) -> p m i e", e=2)
        table_v = table[:].rearrange("p m (i q e) -> p m i q e", q=2, e=2)

        def build_table(i):
            m0, m1 = 4 * i, 4 * i + 4
            nc.vector.tensor_copy(out=table_v[:, m0:m1, :, 0, :], in_=fc_v[:, m0:m1, :, :])
            nc.vector.tensor_scalar(
                out=table_v[:, m0:m1, :, 1, 0], in0=fc_v[:, m0:m1, :, 1], scalar1=-1.0, scalar2=None, op0=MULT
            )
            nc.vector.tensor_copy(out=table_v[:, m0:m1, :, 1, 1], in_=fc_v[:, m0:m1, :, 0])

        def regroup_last_block():
            wci, wcn = find_chunk(W_CODE_CHUNKS, last_n)
            wsi, wsn = find_chunk(W_SCALE_CHUNKS, last_n)
            moves = (
                (wc_last, wc[wci][:, :, 2 * N_TILE * wcn : 2 * N_TILE * (wcn + 1)]),
                (ws_last, ws[wsi][:, :, N_TILE * wsn : N_TILE * (wsn + 1)]),
            )
            for dst, src in moves:
                src_v = src.bitcast(I32).rearrange("p g (h k w) -> p g h k w", h=HEADS, k=2)
                dst_v = dst[:].bitcast(I32).rearrange("p g (k h w) -> p g k h w", k=2, h=HEADS)
                nc.vector.tensor_copy(out=dst_v[:, :, 0, :, :], in_=src_v[:, :, :, 1, :])
                nc.vector.tensor_copy(out=dst_v[:, :, 1, :, :], in_=src_v[:, :, :, 0, :])

        def mx_group(acc, m, n, col0, width):
            xci, xcm = find_chunk(X_CODE_CHUNKS, m)
            xsi, xsm = find_chunk(X_SCALE_CHUNKS, m)
            if n == last_n:
                w_codes, w_scales, code_col, scale_col = wc_last, ws_last, col0, col0
            else:
                wci, wcn = find_chunk(W_CODE_CHUNKS, n)
                wsi, wsn = find_chunk(W_SCALE_CHUNKS, n)
                w_codes, w_scales = wc[wci], ws[wsi]
                code_col, scale_col = N_TILE * wcn + col0, N_TILE * wsn + col0
            for g in range(PASSES):
                nc.tensor.matmul_mx(
                    out=acc,
                    lhsT=xc[xci][:, g, 2 * P * xcm : 2 * P * (xcm + 1)].bitcast(FP4X4),
                    lhsT_scale=xs[xsi][:, g, P * xsm : P * (xsm + 1)],
                    rhs=w_codes[:, g, 2 * code_col : 2 * (code_col + width)].bitcast(FP4X4),
                    rhs_scale=w_scales[:, g, scale_col : scale_col + width],
                    start=(g == 0),
                    stop=(g == PASSES - 1),
                )

        def by_head(ap):
            return ap.rearrange("p (h d) -> p h d", h=HEADS)

        def rope_products(ab_bank, rope, m):
            nc.vector.tensor_tensor(
                out=ab_bank.rearrange("p (h k e) -> p h k e", h=HEADS, e=2),
                in0=rope.unsqueeze(3).to_broadcast([P, HEADS, P, 2]),
                in1=table[:, m, :].rearrange("p (k e) -> p k e", e=2).unsqueeze(1).to_broadcast([P, HEADS, P, 2]),
                op=MULT,
            )

        def rope_sums(engine, ab, o, first, count):
            ab_v = ab[:, first : first + count, :].rearrange("p j (h i q e) -> p (j h) i q e", h=HEADS, q=2, e=2)
            o_v = (
                o[:, first : first + count, :]
                .rearrange("p j (h d) -> p (j h) d", h=HEADS)[:, :, P : 2 * P]
                .rearrange("p a (i e) -> p a i e", e=2)
            )
            engine.tensor_tensor(out=o_v, in0=ab_v[:, :, :, 0, :], in1=ab_v[:, :, :, 1, :], op=ADD)

        def finish_pair(ab, o, m, n):
            rope_sums(nc.gpsimd, ab, o, 0, PAIR)
            nc.sync.dma_start(out=out_v[:, m : m + PAIR, N_TILE * n : N_TILE * (n + 1)], in_=o[:])

        build_table(0)
        pending = None
        ab = None
        o = None
        for j in range(N_BLOCKS * M_TILES - TAIL):
            n, m = divmod(j, M_TILES)
            half = j % PAIR
            acc = psum.tile([P, N_TILE], F32, name="acc")
            mx_group(acc[:], m, n, 0, N_TILE)
            if half == 0:
                ab = prod.tile([P, PAIR, N_TILE], F32, name="ab")
                o = res.tile([P, PAIR, N_TILE], F32, name="o")
            if n == last_n:
                rope, nope = by_head(acc[:, 0 : N_TILE // 2]), by_head(acc[:, N_TILE // 2 : N_TILE])
            else:
                rope, nope = by_head(acc[:])[:, :, P : 2 * P], by_head(acc[:])[:, :, 0:P]
            rope_products(ab[:, half, :], rope, m)
            nc.scalar.copy(out=by_head(o[:, half, :])[:, :, 0:P], in_=nope)
            if pending is not None:
                finish_pair(*pending)
                pending = None
            if half == PAIR - 1:
                pending = (ab, o, m - (PAIR - 1), n)
            if j == N_BLOCKS * M_TILES - TAIL - 1:
                rope_sums(nc.gpsimd, ab, o, 0, 1)
            if n == 0 and m in (1, 5, 9):
                build_table((m + 3) // 4)
            if j in LATER_W:
                nc.vector.memset(ws[LATER_W[j]][:].bitcast(I32), 0)
                load_w_scales(LATER_W[j])
                load_w_codes(LATER_W[j])
            if j == REGROUP_AT:
                regroup_last_block()

        tail = []
        for t in range(TAIL):
            m = M_TILES - TAIL + t
            half = t % PAIR
            acc = psum.tile([P, N_TILE], F32, name="acc")
            mx_group(acc[:, 0 : N_TILE // 2], m, last_n, 0, N_TILE // 2)
            if half == 0:
                ab = prod.tile([P, PAIR, N_TILE], F32, name="ab")
                o = res.tile([P, PAIR, N_TILE], F32, name="o")
            rope_products(ab[:, half, :], by_head(acc[:, 0 : N_TILE // 2]), m)
            if t == 0:
                rope_sums(nc.gpsimd, pending[0], pending[1], 1, 1)
                nc.sync.dma_start(
                    out=out_v[:, pending[2] : pending[2] + PAIR, N_TILE * last_n : N_TILE * (last_n + 1)], in_=pending[1][:]
                )
            else:
                rope_sums(nc.vector, tail[t - 1][0], tail[t - 1][1], tail[t - 1][2], 1)
            tail.append((ab, o, half, m))
        rope_sums(nc.vector, tail[TAIL - 1][0], tail[TAIL - 1][1], tail[TAIL - 1][2], 1)
        for ab, o, half, m in tail:
            acc = psum.tile([P, N_TILE], F32, name="acc")
            mx_group(acc[:, 0 : N_TILE // 2], m, last_n, N_TILE // 2, N_TILE // 2)
            nc.scalar.copy(out=by_head(o[:, half, :])[:, :, 0:P], in_=by_head(acc[:, 0 : N_TILE // 2]))
            nc.sync.dma_start(out=out_v[:, m, N_TILE * last_n : N_TILE * (last_n + 1)], in_=o[:, half, :])
